import numpy as np
import ml_dtypes


def mxq(x, axis, fmt="e4m3"):
    dtype, down = {"e4m3": (ml_dtypes.float8_e4m3fn, 7), "e5m2": (ml_dtypes.float8_e5m2, 14)}[fmt]
    v = np.moveaxis(np.asarray(x, np.float32).astype(ml_dtypes.bfloat16).astype(np.float64), axis, -1)
    blocks = v.reshape(v.shape[:-1] + (-1, 32))
    amax = np.abs(blocks).max(-1, keepdims=True)
    byte = np.maximum(np.where(amax > 0, np.frexp(amax)[1] - 1 + 127, 0) - down, 1)
    scale = np.exp2(byte - 127.0)
    codes = (blocks / scale).astype(np.float32).astype(dtype).astype(np.float64)
    return np.moveaxis((codes * scale).reshape(v.shape), -1, axis)


WIDE = False


def mx_kscale(k):
    if not WIDE:
        return np.ones(k)
    levels = np.array([10, -10, 5, -5, 0])
    a = np.random.permutation(np.resize(levels, k // 512 * 4)).reshape(k // 512, 4)
    idx = np.arange(k)
    return np.exp2(a[idx // 512, idx % 128 // 32])


BF16 = ml_dtypes.bfloat16


def bf(x):
    return np.asarray(x, np.float32).astype(BF16)


def f64(x):
    return np.asarray(x).astype(np.float64)


B, N, D, H, L, C = 4, 512, 512, 8, 3, 2
HD = D // H


def setup_inputs():
    s, t = mx_kscale(D), mx_kscale(D)
    tk = t.reshape(H, HD)[:, :L]
    return {
        "fields": bf((np.random.standard_normal((B, N, D)) + np.random.standard_normal((B, 1, D))) * t),
        "h2": bf(np.maximum(np.random.standard_normal((B, N, D)), 0.0) * 1.4 * s),
        "corr_kernels": bf(np.random.standard_normal((H, L, L)) * 2.5 / tk[:, None, :]),
        "w3": bf(np.random.standard_normal((D, D)) * 1.5 / np.sqrt(D) * t[:, None] / s[None, :]),
        "b3": bf(np.random.standard_normal(D) * 0.3 * t),
        "out_w": bf(np.random.standard_normal((D, D)) / np.sqrt(D) / t[None, :]),
        "out_b": bf(np.random.standard_normal(D) * 0.3),
        "inter_w": bf(1.0 + 0.5 * np.random.standard_normal(C)),
    }


def reference(fields, h2, corr_kernels, w3, b3, out_w, out_b, inter_w):
    f = f64(fields).reshape(B, N, H, HD)
    ck = f64(corr_kernels)
    corr = np.zeros((B, N, H, HD))
    for lag in range(1, L + 1):
        base = f[:, :-lag]
        shifted = f[:, lag:]
        w = np.pad(ck[:, lag - 1, :], ((0, 0), (0, HD - L)))
        mean_shift = shifted.mean(axis=1, keepdims=True)
        cw = base * w[None, None] * mean_shift
        corr = corr + np.pad(cw, ((0, 0), (0, lag), (0, 0), (0, 0)))
    corr = corr / L
    nl = ((mxq(f64(h2), 2, "e4m3") @ mxq(f64(w3), 1, "e4m3").T) + f64(b3)).reshape(B, N, H, HD)
    r = f64(inter_w)
    e = np.exp(r - r.max())
    iw = e / e.sum()
    enhanced = (f + iw[0] * corr + iw[1] * nl).reshape(B, N, D)
    return (mxq(enhanced, 2, "e4m3") @ mxq(f64(out_w), 1, "e4m3").T) + f64(out_b)

@@ -1,0 +1,349 @@
+import concourse.mybir as mybir
+from concourse.masks import make_identity
+
+F32 = mybir.dt.float32
+BF16 = mybir.dt.bfloat16
+U32 = mybir.dt.uint32
+U8 = mybir.dt.uint8
+FP8X4 = mybir.dt.float8_e4m3fn_x4
+ALU = mybir.AluOpType
+ACT = mybir.ActivationFunctionType
+AXIS = mybir.AxisListType
+
+B, N, D, H, L = 4, 512, 512, 8, 3
+HD = D // H
+P = 128
+PACK = 4
+TILES = 4
+
+FLOPS = 2 * 2 * B * N * D * D
+
+
+def word_columns(rows, u):
+    return rows.bitcast(F32).rearrange("r (p u) -> r u p", u=2)[:, u, :]
+
+
+def flip_rows(nc, copy_out, psum_flip, stage, ident_f32, rows4):
+    grouped = stage.tile([P, TILES, P, PACK], BF16, align_bytes=64)
+    grouped_words = grouped[:].bitcast(F32)
+    for pair in range(TILES // 2):
+        flipped = psum_flip.tile([P, 2, 2, P], F32)
+        for g in range(2):
+            for u in range(2):
+                nc.tensor.transpose(
+                    flipped[:, g, u, :], word_columns(rows4[:, 2 * pair + g, :], u), ident_f32[:]
+                )
+        copy_out(
+            out=grouped_words[:, 2 * pair : 2 * pair + 2, :, :],
+            in_=flipped[:].rearrange("p g u r -> p g r u"),
+        )
+    return grouped
+
+
+def quantise_rows(nc, grouped, codes, scales):
+    nc.vector.quantize_mx(
+        out=codes.bitcast(FP8X4), scales=scales, in_=grouped[:].rearrange("p g r t -> p (g r t)")
+    )
+
+
+def tile_fieldinteractionoperators_pa_kernel(
+    tc, fields, h2, corr_kernels, w3, b3, out_w, out_b, inter_w, out
+):
+    nc = tc.nc
+    with (
+        tc.tile_pool(name="keep", bufs=1) as keep,
+        tc.tile_pool(name="stage", bufs=2) as stage,
+        tc.tile_pool(name="results", bufs=3) as results,
+        tc.psum_pool(name="psum_flip", bufs=2) as psum_flip,
+        tc.psum_pool(name="psum_field", bufs=2) as psum_field,
+        tc.psum_pool(name="psum_first", bufs=2) as psum_first,
+        tc.psum_pool(name="psum_second", bufs=2) as psum_second,
+    ):
+        ident_f32 = keep.tile([P, P], F32)
+        make_identity(nc, ident_f32[:])
+        ident_bf16 = keep.tile([P, P], BF16)
+        make_identity(nc, ident_bf16[:])
+        ones = keep.tile([P, P], BF16)
+        nc.vector.memset(ones[:], 1.0)
+        ones_but_first = keep.tile([P, P], BF16)
+        nc.vector.memset(ones_but_first[:], 1.0)
+        nc.vector.memset(ones_but_first[0:1, :], 0.0)
+        out_b_row = keep.tile([P, D], BF16)
+        nc.vector.memset(out_b_row[:], 0.0)
+
+        kernels_all = keep.tile([P, H, L, L], BF16)
+        nc.scalar.dma_start(
+            out=kernels_all[:].rearrange("p h l j -> p (h l j)"),
+            in_=corr_kernels.rearrange("h l j -> (h l j)").partition_broadcast(P),
+        )
+        mix = keep.tile([P, 2], BF16)
+        nc.scalar.dma_start(out=mix[:], in_=inter_w.partition_broadcast(P))
+        b3_pt = keep.tile([P, PACK], BF16)
+        nc.scalar.dma_start(out=b3_pt[:], in_=b3.rearrange("(p t) -> p t", t=PACK))
+        nc.scalar.dma_start(out=out_b_row[0:1, :], in_=out_b.unsqueeze(0))
+
+        f_nat = keep.tile([P, B, TILES, D], BF16)
+        h_nat = keep.tile([P, B, TILES, D], BF16)
+        w3_nat = keep.tile([P, TILES, D], BF16)
+        ow_nat = keep.tile([P, TILES, D], BF16)
+
+        def load_tokens(tile, tensor, b):
+            nc.sync.dma_start(out=tile[:, b], in_=tensor[b].rearrange("(q i) c -> q i c", i=TILES))
+
+        load_tokens(f_nat, fields, 0)
+        nc.sync.dma_start(out=w3_nat[:], in_=w3.rearrange("(p t) k -> p t k", t=TILES))
+        load_tokens(h_nat, h2, 0)
+        nc.sync.dma_start(out=ow_nat[:], in_=out_w.rearrange("(g r) c -> r g c", r=P))
+        for b in range(1, B):
+            load_tokens(f_nat, fields, b)
+        for b in range(1, B):
+            load_tokens(h_nat, h2, b)
+
+        neg_top = keep.tile([P, 1], F32)
+        nc.vector.tensor_max(out=neg_top[:], in0=mix[:, 0:1], in1=mix[:, 1:2])
+        nc.vector.tensor_scalar_mul(out=neg_top[:], in0=neg_top[:], scalar1=-1.0)
+        expd = keep.tile([P, 2], F32)
+        total = keep.tile([P, 1], F32)
+        nc.scalar.activation(out=expd[:], in_=mix[:], func=ACT.Exp, bias=neg_top[:, 0:1], scale=1.0, accum_out=total[:])
+        nc.vector.reciprocal(out=total[:], in_=total[:])
+        iw = keep.tile([P, 2], F32)
+        nc.vector.tensor_scalar_mul(out=iw[:], in0=expd[:], scalar1=total[:, 0:1])
+
+        bias_pt = keep.tile([P, PACK], F32)
+        nc.vector.tensor_scalar_mul(out=bias_pt[:], in0=b3_pt[:], scalar1=iw[:, 1:2])
+
+        weight = keep.tile([P, L, H * L], F32)
+        for s in range(L):
+            lag = L - s
+            nc.vector.tensor_scalar_mul(
+                out=weight[:, s, :].rearrange("p (h j) -> p h j", j=L),
+                in0=kernels_all[:, :, lag - 1, :],
+                scalar1=1.0 / (L * (N - lag)),
+            )
+        own_head = ident_f32[:].rearrange("p (h r) -> p h r", r=P // H)[:, :, 0]
+
+        gain = keep.tile([P, B, L], F32)
+        lacking = keep.tile([P, B, L, L], F32)
+
+        def find_gains(first, count):
+            batches = slice(first, first + count)
+
+            def head_starts(i):
+                return f_nat[:, batches, i, :].rearrange("q b (h j) -> q b h j", j=HD)[:, :, :, 0:L]
+
+            sums = psum_flip.tile([P, 2, L, count, H, L], F32, tag="flipped")
+            shifted = sums[:, 0]
+            for s in range(L):
+                lag = L - s
+                for i in range(TILES):
+                    nc.tensor.matmul(
+                        out=shifted[:, s],
+                        lhsT=ones[:] if i >= lag else ones_but_first[:],
+                        rhs=head_starts(i),
+                        start=(i == 0),
+                        stop=(i == TILES - 1),
+                    )
+            last = sums[:, 1]
+            for s in range(L):
+                nc.tensor.matmul(
+                    out=last[:, s],
+                    lhsT=ident_bf16[:, P - 1 : P].to_broadcast([P, P]),
+                    rhs=head_starts(s + 1),
+                    start=True,
+                    stop=True,
+                )
+            term = stage.tile([P, L, count, H * L], F32)
+            nc.vector.tensor_tensor(
+                out=term[:],
+                in0=shifted.rearrange("p s b h j -> p s b (h j)"),
+                in1=weight[:].unsqueeze(2).to_broadcast([P, L, count, H * L]),
+                op=ALU.mult,
+            )
+            for s in range(1, L):
+                nc.vector.tensor_add(out=term[:, s], in0=term[:, s], in1=term[:, s - 1])
+            picked = stage.tile([P, L * count, L, H], F32)
+            nc.vector.tensor_tensor(
+                out=picked[:],
+                in0=term[:].rearrange("p s b (h j) -> p (s b) j h", j=L),
+                in1=own_head.unsqueeze(1).unsqueeze(1).to_broadcast([P, L * count, L, H]),
+                op=ALU.mult,
+            )
+            nc.vector.tensor_reduce(
+                out=gain[:, batches], in_=picked[:, (L - 1) * count : L * count], axis=AXIS.X, op=ALU.add
+            )
+            nc.vector.tensor_scalar(
+                out=gain[:, batches], in0=gain[:, batches], scalar1=iw[:, 0:1], scalar2=1.0, op0=ALU.mult, op1=ALU.add
+            )
+            lacking_by_head = stage.tile([P, L * count, L, H], F32)
+            nc.vector.tensor_tensor(
+                out=lacking_by_head[:], in0=last.rearrange("p s b h j -> p (s b) j h"), in1=picked[:], op=ALU.mult
+            )
+            nc.vector.tensor_reduce(
+                out=lacking[:, batches].rearrange("p b s t -> p s b t"),
+                in_=lacking_by_head[:].rearrange("p (s b) t h -> p s b t h", b=count),
+                axis=AXIS.X,
+                op=ALU.add,
+            )
+            nc.vector.tensor_scalar_mul(out=lacking[:, batches], in0=lacking[:, batches], scalar1=iw[:, 0:1])
+
+        field_banks = {}
+        scaled = {}
+        h_grouped = {}
+        h_codes = {}
+        h_scales = {}
+
+        def flip_fields(b):
+            for u in range(2):
+                flipped_f = psum_field.tile([P, TILES, P], F32)
+                for i in range(TILES):
+                    nc.tensor.transpose(flipped_f[:, i, :], word_columns(f_nat[:, b, i, :], u), ident_f32[:])
+                field_banks[(b, u)] = flipped_f
+            scaled_b = stage.tile([P, PACK, N], F32)
+            scaled[b] = scaled_b
+
+        def scale_fields(b, u):
+            halves = field_banks[(b, u)][:].bitcast(BF16).rearrange("p i (q e) -> p (i q) e", e=2)
+            for e in range(2):
+                t = 2 * u + e
+                nc.scalar.activation(
+                    out=scaled[b][:, t, :],
+                    in_=halves[:, :, e],
+                    func=ACT.Identity,
+                    scale=gain[:, b, t : t + 1] if t < L else 1.0,
+                    bias=bias_pt[:, t : t + 1],
+                )
+
+        def mend_last_tokens(b):
+            last_columns = scaled[b][:, 0:L, :].rearrange("p t (i q) -> p t i q", q=P)[:, :, 1:TILES, P - 1]
+            nc.vector.tensor_tensor(
+                out=last_columns, in0=last_columns, in1=lacking[:, b].rearrange("p s t -> p t s"), op=ALU.subtract
+            )
+
+        def flip_hidden(b):
+            h_grouped[b] = flip_rows(nc, nc.scalar.copy, psum_flip, stage, ident_f32, h_nat[:, b])
+
+        def quantise_hidden(b):
+            codes = stage.tile([P, N], U32, align_bytes=64)
+            planes = stage.tile([P, N], U8, align_bytes=64)
+            quantise_rows(nc, h_grouped[b], codes[:], planes[:])
+            h_codes[b], h_scales[b] = codes, planes
+
+        def prepare(b, part):
+            if part == 0:
+                flip_fields(b)
+                scale_fields(b, 0)
+            if part == 1:
+                flip_hidden(b)
+            if part == 2:
+                scale_fields(b, 1)
+                quantise_hidden(b)
+            if part == 3:
+                mend_last_tokens(b)
+
+        nl = {}
+        enhanced = {}
+        e_codes = {}
+        e_scales = {}
+        acc = {}
+        result = {}
+
+        def first_product(g):
+            b, i = divmod(g, TILES)
+            tokens = slice(i * P, (i + 1) * P)
+            bank = psum_first.tile([P, PACK, P], F32)
+            for t in range(PACK):
+                channels = slice(t * P, (t + 1) * P)
+                nc.tensor.matmul_mx(
+                    out=bank[:, t, :],
+                    lhsT=w3_codes[:, channels].bitcast(FP8X4),
+                    lhsT_scale=w3_scales[:, channels],
+                    rhs=h_codes[b][:, tokens].bitcast(FP8X4),
+                    rhs_scale=h_scales[b][:, tokens],
+                    start=True,
+                    stop=True,
+                )
+            nl[g] = bank
+
+        def fuse(g):
+            b, i = divmod(g, TILES)
+            fused = results.tile([P, P, PACK], BF16, align_bytes=64)
+            nc.vector.scalar_tensor_tensor(
+                out=fused[:],
+                in0=nl[g][:].rearrange("p t q -> p q t"),
+                scalar=iw[:, 1:2],
+                in1=scaled[b][:, :, i * P : (i + 1) * P].rearrange("p t q -> p q t"),
+                op0=ALU.mult,
+                op1=ALU.add,
+            )
+            enhanced[g] = fused
+
+        def quantise_enhanced(g):
+            codes = results.tile([P, P], U32, align_bytes=64)
+            planes = results.tile([P, P], U8, align_bytes=64)
+            nc.vector.quantize_mx(
+                out=codes[:].bitcast(FP8X4), scales=planes[:], in_=enhanced[g][:].rearrange("p q t -> p (q t)")
+            )
+            e_codes[g], e_scales[g] = codes, planes
+
+        def second_product(g):
+            bank = psum_second.tile([P, D], F32)
+            nc.tensor.matmul_mx(
+                out=bank[:],
+                lhsT=e_codes[g][:].bitcast(FP8X4),
+                lhsT_scale=e_scales[g][:],
+                rhs=ow_codes[:].bitcast(FP8X4),
+                rhs_scale=ow_scales[:],
+                start=True,
+                stop=True,
+            )
+            acc[g] = bank
+
+        def finish(g):
+            b, i = divmod(g, TILES)
+            if i % 2 == 0:
+                both = results.tile([P, 2, D], F32)
+                result[g + 1] = both
+                nc.scalar.copy(out=both[:, 0, :], in_=acc[g][:])
+                nc.gpsimd.tensor_tensor(out=both[:, 0, :], in0=both[:, 0, :], in1=out_b_all[:], op=ALU.add)
+            else:
+                nc.vector.tensor_tensor(out=result[g][:, 1, :], in0=acc[g][:], in1=out_b_all[:], op=ALU.add)
+                nc.sync.dma_start(
+                    out=out[b].rearrange("(q i) o -> q i o", i=TILES)[:, i - 1 : i + 1, :], in_=result[g][:]
+                )
+
+        flip_fields(0)
+        find_gains(0, 1)
+        w3_codes = keep.tile([P, D], U32, align_bytes=64)
+        w3_scales = keep.tile([P, D], U8, align_bytes=64)
+        w3_grouped = flip_rows(nc, nc.vector.tensor_copy, psum_flip, stage, ident_f32, w3_nat[:])
+        quantise_rows(nc, w3_grouped, w3_codes[:], w3_scales[:])
+        scale_fields(0, 0)
+        flip_hidden(0)
+        scale_fields(0, 1)
+        ow_codes = keep.tile([P, D], U32, align_bytes=64)
+        ow_scales = keep.tile([P, D], U8, align_bytes=64)
+        ow_grouped = flip_rows(nc, nc.vector.tensor_copy, psum_flip, stage, ident_f32, ow_nat[:])
+        quantise_hidden(0)
+        first_product(0)
+        quantise_rows(nc, ow_grouped, ow_codes[:], ow_scales[:])
+        spread_out_b = psum_second.tile([P, D], F32, tag="bank")
+        nc.tensor.matmul(out=spread_out_b[:], lhsT=ones[:], rhs=out_b_row[:], start=True, stop=True)
+        out_b_all = keep.tile([P, D], F32)
+        nc.scalar.copy(out=out_b_all[:], in_=spread_out_b[:])
+        mend_last_tokens(0)
+
+        ALL = B * TILES
+        for g in range(ALL + 2):
+            if g < ALL:
+                fuse(g)
+            if g + 1 < ALL:
+                first_product(g + 1)
+            if 0 <= g - 1 < ALL:
+                quantise_enhanced(g - 1)
+                second_product(g - 1)
+            if 0 <= g - 2 < ALL:
+                finish(g - 2)
+            if g == 0:
+                find_gains(1, B - 1)
+            if g // TILES + 1 < B:
+                prepare(g // TILES + 1, g % TILES)

@@ -58,6 +58,7 @@ def tile_fieldinteractionoperators_pa_kernel(
         tc.psum_pool(name="psum_field", bufs=2) as psum_field,
         tc.psum_pool(name="psum_first", bufs=2) as psum_first,
         tc.psum_pool(name="psum_second", bufs=2) as psum_second,
+        tc.manual_schedule(),
     ):
         ident_f32 = keep.tile([P, P], F32)
         make_identity(nc, ident_f32[:])

@@ -15,35 +15,41 @@ HD = D // H
 P = 128
 PACK = 4
 TILES = 4
+ALL = B * TILES
+SCALAR_TILES = (0, 2)
 
 FLOPS = 2 * 2 * B * N * D * D
 
 
-def word_columns(rows, u):
+def near_words(rows, u):
+    return rows.bitcast(F32)[:, u * P : (u + 1) * P]
+
+
+def alternate_words(rows, u):
     return rows.bitcast(F32).rearrange("r (p u) -> r u p", u=2)[:, u, :]
 
 
-def flip_rows(nc, copy_out, psum_flip, stage, ident_f32, rows4):
-    grouped = stage.tile([P, TILES, P, PACK], BF16, align_bytes=64)
-    grouped_words = grouped[:].bitcast(F32)
-    for pair in range(TILES // 2):
-        flipped = psum_flip.tile([P, 2, 2, P], F32)
-        for g in range(2):
-            for u in range(2):
-                nc.tensor.transpose(
-                    flipped[:, g, u, :], word_columns(rows4[:, 2 * pair + g, :], u), ident_f32[:]
-                )
-        copy_out(
-            out=grouped_words[:, 2 * pair : 2 * pair + 2, :, :],
-            in_=flipped[:].rearrange("p g u r -> p g r u"),
-        )
-    return grouped
+def flip_two_row_tiles(nc, bank, rows2, words, ident_f32):
+    for g in range(2):
+        for u in range(2):
+            nc.tensor.transpose(bank[:, g, u, :], words(rows2[:, g, :], u), ident_f32[:])
+
+
+def copy_two_row_tiles(copy_out, grouped, pair, bank):
+    copy_out(
+        out=grouped[:].bitcast(F32)[:, 2 * pair : 2 * pair + 2, :, :], in_=bank[:].rearrange("p g u r -> p g r u")
+    )
 
 
 def quantise_rows(nc, grouped, codes, scales):
     nc.vector.quantize_mx(
         out=codes.bitcast(FP8X4), scales=scales, in_=grouped[:].rearrange("p g r t -> p (g r t)")
     )
+
+
+def batch_due(g, lead):
+    b, rest = divmod(g + lead, TILES)
+    return b if rest == 0 and b < B else None
 
 
 def tile_fieldinteractionoperators_pa_kernel(
@@ -53,7 +59,7 @@ def tile_fieldinteractionoperators_pa_kernel(
     with (
         tc.tile_pool(name="keep", bufs=1) as keep,
         tc.tile_pool(name="stage", bufs=2) as stage,
-        tc.tile_pool(name="results", bufs=3) as results,
+        tc.tile_pool(name="results", bufs=4) as results,
         tc.psum_pool(name="psum_flip", bufs=2) as psum_flip,
         tc.psum_pool(name="psum_field", bufs=2) as psum_field,
         tc.psum_pool(name="psum_first", bufs=2) as psum_first,
@@ -62,8 +68,6 @@ def tile_fieldinteractionoperators_pa_kernel(
     ):
         ident_f32 = keep.tile([P, P], F32)
         make_identity(nc, ident_f32[:])
-        ident_bf16 = keep.tile([P, P], BF16)
-        make_identity(nc, ident_bf16[:])
         ones = keep.tile([P, P], BF16)
         nc.vector.memset(ones[:], 1.0)
         ones_but_first = keep.tile([P, P], BF16)
@@ -71,18 +75,12 @@ def tile_fieldinteractionoperators_pa_kernel(
         nc.vector.memset(ones_but_first[0:1, :], 0.0)
         out_b_row = keep.tile([P, D], BF16)
         nc.vector.memset(out_b_row[:], 0.0)
+        zero = keep.tile([P, 1], F32)
+        nc.vector.memset(zero[:], 0.0)
 
         kernels_all = keep.tile([P, H, L, L], BF16)
-        nc.scalar.dma_start(
-            out=kernels_all[:].rearrange("p h l j -> p (h l j)"),
-            in_=corr_kernels.rearrange("h l j -> (h l j)").partition_broadcast(P),
-        )
         mix = keep.tile([P, 2], BF16)
-        nc.scalar.dma_start(out=mix[:], in_=inter_w.partition_broadcast(P))
         b3_pt = keep.tile([P, PACK], BF16)
-        nc.scalar.dma_start(out=b3_pt[:], in_=b3.rearrange("(p t) -> p t", t=PACK))
-        nc.scalar.dma_start(out=out_b_row[0:1, :], in_=out_b.unsqueeze(0))
-
         f_nat = keep.tile([P, B, TILES, D], BF16)
         h_nat = keep.tile([P, B, TILES, D], BF16)
         w3_nat = keep.tile([P, TILES, D], BF16)
@@ -91,14 +89,23 @@ def tile_fieldinteractionoperators_pa_kernel(
         def load_tokens(tile, tensor, b):
             nc.sync.dma_start(out=tile[:, b], in_=tensor[b].rearrange("(q i) c -> q i c", i=TILES))
 
+        nc.scalar.dma_start(
+            out=kernels_all[:].rearrange("p h l j -> p (h l j)"),
+            in_=corr_kernels.rearrange("h l j -> (h l j)").partition_broadcast(P),
+        )
+        nc.scalar.dma_start(out=mix[:], in_=inter_w.partition_broadcast(P))
+        nc.scalar.dma_start(out=b3_pt[:], in_=b3.rearrange("(p t) -> p t", t=PACK))
+        nc.scalar.dma_start(out=out_b_row[0:1, :], in_=out_b.unsqueeze(0))
         load_tokens(f_nat, fields, 0)
         nc.sync.dma_start(out=w3_nat[:], in_=w3.rearrange("(p t) k -> p t k", t=TILES))
         load_tokens(h_nat, h2, 0)
         nc.sync.dma_start(out=ow_nat[:], in_=out_w.rearrange("(g r) c -> r g c", r=P))
         for b in range(1, B):
             load_tokens(f_nat, fields, b)
-        for b in range(1, B):
             load_tokens(h_nat, h2, b)
+
+        warm = keep.tile([P, 1], F32)
+        nc.scalar.activation(out=warm[:], in_=zero[:], func=ACT.Exp)
 
         neg_top = keep.tile([P, 1], F32)
         nc.vector.tensor_max(out=neg_top[:], in0=mix[:, 0:1], in1=mix[:, 1:2])
@@ -106,140 +113,138 @@ def tile_fieldinteractionoperators_pa_kernel(
         expd = keep.tile([P, 2], F32)
         total = keep.tile([P, 1], F32)
         nc.scalar.activation(out=expd[:], in_=mix[:], func=ACT.Exp, bias=neg_top[:, 0:1], scale=1.0, accum_out=total[:])
+
+        own_head = ident_f32[:].rearrange("p (h r) -> p h r", r=P // H)[:, :, 0]
+        pick = keep.tile([P, L, L + 1, L, H], F32)
+        nc.vector.memset(pick[:], 0.0)
+        for s in range(L):
+            lag = L - s
+            nc.vector.scalar_tensor_tensor(
+                out=pick[:, :, L, s, :],
+                in0=kernels_all[:, :, lag - 1, :].rearrange("p h j -> p j h"),
+                scalar=1.0 / (L * (N - lag)),
+                in1=own_head.unsqueeze(1).to_broadcast([P, L, H]),
+                op0=ALU.mult,
+                op1=ALU.mult,
+            )
+        for a in range(L):
+            nc.vector.tensor_copy(out=pick[:, :, a, 0 : a + 1, :], in_=pick[:, :, L, 0 : a + 1, :])
+        one_if_whole = keep.tile([P, L, L + 1], F32)
+        nc.vector.memset(one_if_whole[:], 0.0)
+        nc.vector.memset(one_if_whole[:, :, L : L + 1], 1.0)
+
         nc.vector.reciprocal(out=total[:], in_=total[:])
         iw = keep.tile([P, 2], F32)
         nc.vector.tensor_scalar_mul(out=iw[:], in0=expd[:], scalar1=total[:, 0:1])
-
         bias_pt = keep.tile([P, PACK], F32)
         nc.vector.tensor_scalar_mul(out=bias_pt[:], in0=b3_pt[:], scalar1=iw[:, 1:2])
 
-        weight = keep.tile([P, L, H * L], F32)
-        for s in range(L):
-            lag = L - s
-            nc.vector.tensor_scalar_mul(
-                out=weight[:, s, :].rearrange("p (h j) -> p h j", j=L),
-                in0=kernels_all[:, :, lag - 1, :],
-                scalar1=1.0 / (L * (N - lag)),
-            )
-        own_head = ident_f32[:].rearrange("p (h r) -> p h r", r=P // H)[:, :, 0]
+        gains = keep.tile([P, B, L, L + 1], F32)
+        sums = {}
 
-        gain = keep.tile([P, B, L], F32)
-        lacking = keep.tile([P, B, L, L], F32)
-
-        def find_gains(first, count):
-            batches = slice(first, first + count)
-
-            def head_starts(i):
-                return f_nat[:, batches, i, :].rearrange("q b (h j) -> q b h j", j=HD)[:, :, :, 0:L]
-
-            sums = psum_flip.tile([P, 2, L, count, H, L], F32, tag="flipped")
-            shifted = sums[:, 0]
+        def sum_fields(b):
+            bank = psum_flip.tile([P, L * H, L], F32, tag="flipped")
             for s in range(L):
                 lag = L - s
                 for i in range(TILES):
                     nc.tensor.matmul(
-                        out=shifted[:, s],
+                        out=bank[:, s * H : (s + 1) * H, :],
                         lhsT=ones[:] if i >= lag else ones_but_first[:],
-                        rhs=head_starts(i),
+                        rhs=f_nat[:, b, i, :].rearrange("q (h j) -> q h j", j=HD)[:, :, 0:L],
                         start=(i == 0),
                         stop=(i == TILES - 1),
                     )
-            last = sums[:, 1]
-            for s in range(L):
-                nc.tensor.matmul(
-                    out=last[:, s],
-                    lhsT=ident_bf16[:, P - 1 : P].to_broadcast([P, P]),
-                    rhs=head_starts(s + 1),
-                    start=True,
-                    stop=True,
-                )
-            term = stage.tile([P, L, count, H * L], F32)
+            sums[b] = bank
+
+        def find_gains(b):
+            terms = stage.tile([P, L, L + 1, L * H], F32, tag="terms")
             nc.vector.tensor_tensor(
-                out=term[:],
-                in0=shifted.rearrange("p s b h j -> p s b (h j)"),
-                in1=weight[:].unsqueeze(2).to_broadcast([P, L, count, H * L]),
+                out=terms[:],
+                in0=sums[b][:].rearrange("p x j -> p j x").unsqueeze(2).to_broadcast([P, L, L + 1, L * H]),
+                in1=pick[:].rearrange("p j a s h -> p j a (s h)"),
                 op=ALU.mult,
             )
-            for s in range(1, L):
-                nc.vector.tensor_add(out=term[:, s], in0=term[:, s], in1=term[:, s - 1])
-            picked = stage.tile([P, L * count, L, H], F32)
-            nc.vector.tensor_tensor(
-                out=picked[:],
-                in0=term[:].rearrange("p s b (h j) -> p (s b) j h", j=L),
-                in1=own_head.unsqueeze(1).unsqueeze(1).to_broadcast([P, L * count, L, H]),
-                op=ALU.mult,
+            factors = stage.tile([P, L, L + 1], F32, tag="factors")
+            nc.vector.tensor_reduce(out=factors[:], in_=terms[:], axis=AXIS.X, op=ALU.add)
+            nc.vector.scalar_tensor_tensor(
+                out=gains[:, b], in0=factors[:], scalar=iw[:, 0:1], in1=one_if_whole[:], op0=ALU.mult, op1=ALU.add
             )
-            nc.vector.tensor_reduce(
-                out=gain[:, batches], in_=picked[:, (L - 1) * count : L * count], axis=AXIS.X, op=ALU.add
-            )
-            nc.vector.tensor_scalar(
-                out=gain[:, batches], in0=gain[:, batches], scalar1=iw[:, 0:1], scalar2=1.0, op0=ALU.mult, op1=ALU.add
-            )
-            lacking_by_head = stage.tile([P, L * count, L, H], F32)
-            nc.vector.tensor_tensor(
-                out=lacking_by_head[:], in0=last.rearrange("p s b h j -> p (s b) j h"), in1=picked[:], op=ALU.mult
-            )
-            nc.vector.tensor_reduce(
-                out=lacking[:, batches].rearrange("p b s t -> p s b t"),
-                in_=lacking_by_head[:].rearrange("p (s b) t h -> p s b t h", b=count),
-                axis=AXIS.X,
-                op=ALU.add,
-            )
-            nc.vector.tensor_scalar_mul(out=lacking[:, batches], in0=lacking[:, batches], scalar1=iw[:, 0:1])
 
         field_banks = {}
         scaled = {}
+        lacking = {}
+        hidden_banks = {}
         h_grouped = {}
         h_codes = {}
         h_scales = {}
 
         def flip_fields(b):
             for u in range(2):
-                flipped_f = psum_field.tile([P, TILES, P], F32)
+                flipped_f = psum_field.tile([P, TILES, P], F32, tag="fields")
                 for i in range(TILES):
-                    nc.tensor.transpose(flipped_f[:, i, :], word_columns(f_nat[:, b, i, :], u), ident_f32[:])
+                    nc.tensor.transpose(flipped_f[:, i, :], alternate_words(f_nat[:, b, i, :], u), ident_f32[:])
                 field_banks[(b, u)] = flipped_f
-            scaled_b = stage.tile([P, PACK, N], F32)
+            scaled_b = stage.tile([P, PACK, N], F32, tag="scaled")
             scaled[b] = scaled_b
 
-        def scale_fields(b, u):
+        def scale_fields(b, t):
+            u, e = divmod(t, 2)
             halves = field_banks[(b, u)][:].bitcast(BF16).rearrange("p i (q e) -> p (i q) e", e=2)
-            for e in range(2):
-                t = 2 * u + e
-                nc.scalar.activation(
-                    out=scaled[b][:, t, :],
-                    in_=halves[:, :, e],
-                    func=ACT.Identity,
-                    scale=gain[:, b, t : t + 1] if t < L else 1.0,
-                    bias=bias_pt[:, t : t + 1],
+            nc.scalar.activation(
+                out=scaled[b][:, t, :],
+                in_=halves[:, :, e],
+                func=ACT.Identity,
+                scale=gains[:, b, t, L : L + 1] if t < L else 1.0,
+                bias=bias_pt[:, t : t + 1],
+            )
+
+        def find_lacking(b):
+            lack = stage.tile([P, L, L], F32, tag="lacking")
+            for u in range(2):
+                count = min(2, L - 2 * u)
+                halves = field_banks[(b, u)][:].bitcast(BF16).rearrange("p i (q e) -> p e i q", e=2)
+                nc.vector.tensor_tensor(
+                    out=lack[:, 2 * u : 2 * u + count, :],
+                    in0=halves[:, 0:count, 1:TILES, P - 1],
+                    in1=gains[:, b, 2 * u : 2 * u + count, 0:L],
+                    op=ALU.mult,
                 )
+            lacking[b] = lack
 
         def mend_last_tokens(b):
             last_columns = scaled[b][:, 0:L, :].rearrange("p t (i q) -> p t i q", q=P)[:, :, 1:TILES, P - 1]
-            nc.vector.tensor_tensor(
-                out=last_columns, in0=last_columns, in1=lacking[:, b].rearrange("p s t -> p t s"), op=ALU.subtract
-            )
+            nc.vector.tensor_tensor(out=last_columns, in0=last_columns, in1=lacking[b][:], op=ALU.subtract)
 
         def flip_hidden(b):
-            h_grouped[b] = flip_rows(nc, nc.scalar.copy, psum_flip, stage, ident_f32, h_nat[:, b])
+            for pair in range(2):
+                bank = psum_flip.tile([P, 2, 2, P], F32, tag="flipped")
+                flip_two_row_tiles(nc, bank, h_nat[:, b, 2 * pair : 2 * pair + 2, :], near_words, ident_f32)
+                hidden_banks[(b, pair)] = bank
+            grouped = stage.tile([P, TILES, P, PACK], BF16, align_bytes=64, tag="grouped")
+            h_grouped[b] = grouped
+
+        def copy_hidden(b, pair):
+            copy_two_row_tiles(nc.scalar.copy, h_grouped[b], pair, hidden_banks[(b, pair)])
 
         def quantise_hidden(b):
-            codes = stage.tile([P, N], U32, align_bytes=64)
-            planes = stage.tile([P, N], U8, align_bytes=64)
+            codes = stage.tile([P, N], U32, align_bytes=64, tag="h_codes")
+            planes = stage.tile([P, N], U8, align_bytes=64, tag="h_scales")
             quantise_rows(nc, h_grouped[b], codes[:], planes[:])
             h_codes[b], h_scales[b] = codes, planes
 
-        def prepare(b, part):
-            if part == 0:
-                flip_fields(b)
-                scale_fields(b, 0)
-            if part == 1:
-                flip_hidden(b)
-            if part == 2:
-                scale_fields(b, 1)
-                quantise_hidden(b)
-            if part == 3:
-                mend_last_tokens(b)
+        def flip_weight(pool, tag, rows4, words):
+            banks = []
+            for pair in range(2):
+                bank = pool.tile([P, 2, 2, P], F32, tag=tag, name="weight_bank")
+                flip_two_row_tiles(nc, bank, rows4[:, 2 * pair : 2 * pair + 2, :], words, ident_f32)
+                banks.append(bank)
+            return banks
+
+        def copy_weight(banks):
+            grouped = stage.tile([P, TILES, P, PACK], BF16, align_bytes=64, tag="grouped")
+            for pair in range(2):
+                copy_two_row_tiles(nc.vector.tensor_copy, grouped, pair, banks[pair])
+            return grouped
 
         nl = {}
         enhanced = {}
@@ -251,7 +256,7 @@ def tile_fieldinteractionoperators_pa_kernel(
         def first_product(g):
             b, i = divmod(g, TILES)
             tokens = slice(i * P, (i + 1) * P)
-            bank = psum_first.tile([P, PACK, P], F32)
+            bank = psum_first.tile([P, PACK, P], F32, tag="nl")
             for t in range(PACK):
                 channels = slice(t * P, (t + 1) * P)
                 nc.tensor.matmul_mx(
@@ -267,7 +272,7 @@ def tile_fieldinteractionoperators_pa_kernel(
 
         def fuse(g):
             b, i = divmod(g, TILES)
-            fused = results.tile([P, P, PACK], BF16, align_bytes=64)
+            fused = results.tile([P, P, PACK], BF16, align_bytes=64, tag="fused")
             nc.vector.scalar_tensor_tensor(
                 out=fused[:],
                 in0=nl[g][:].rearrange("p t q -> p q t"),
@@ -279,15 +284,15 @@ def tile_fieldinteractionoperators_pa_kernel(
             enhanced[g] = fused
 
         def quantise_enhanced(g):
-            codes = results.tile([P, P], U32, align_bytes=64)
-            planes = results.tile([P, P], U8, align_bytes=64)
+            codes = results.tile([P, P], U32, align_bytes=64, tag="e_codes")
+            planes = results.tile([P, P], U8, align_bytes=64, tag="e_scales")
             nc.vector.quantize_mx(
                 out=codes[:].bitcast(FP8X4), scales=planes[:], in_=enhanced[g][:].rearrange("p q t -> p (q t)")
             )
             e_codes[g], e_scales[g] = codes, planes
 
         def second_product(g):
-            bank = psum_second.tile([P, D], F32)
+            bank = psum_second.tile([P, D], F32, tag="acc")
             nc.tensor.matmul_mx(
                 out=bank[:],
                 lhsT=e_codes[g][:].bitcast(FP8X4),
@@ -302,49 +307,81 @@ def tile_fieldinteractionoperators_pa_kernel(
         def finish(g):
             b, i = divmod(g, TILES)
             if i % 2 == 0:
-                both = results.tile([P, 2, D], F32)
-                result[g + 1] = both
-                nc.scalar.copy(out=both[:, 0, :], in_=acc[g][:])
-                nc.gpsimd.tensor_tensor(out=both[:, 0, :], in0=both[:, 0, :], in1=out_b_all[:], op=ALU.add)
+                both = results.tile([P, 2, D], F32, tag="both")
+                result[g] = result[g + 1] = both
+            mine = result[g][:, i % 2, :]
+            if i in SCALAR_TILES:
+                nc.scalar.copy(out=mine, in_=acc[g][:])
+                nc.gpsimd.tensor_tensor(out=mine, in0=mine, in1=out_b_all[:], op=ALU.add)
             else:
-                nc.vector.tensor_tensor(out=result[g][:, 1, :], in0=acc[g][:], in1=out_b_all[:], op=ALU.add)
+                nc.vector.tensor_tensor(out=mine, in0=acc[g][:], in1=out_b_all[:], op=ALU.add)
+            if i % 2 == 1:
                 nc.sync.dma_start(
                     out=out[b].rearrange("(q i) o -> q i o", i=TILES)[:, i - 1 : i + 1, :], in_=result[g][:]
                 )
 
+        sum_fields(0)
+        find_gains(0)
         flip_fields(0)
-        find_gains(0, 1)
+        w3_banks = flip_weight(psum_first, "nl", w3_nat[:], near_words)
+        w3_grouped = copy_weight(w3_banks)
+        flip_hidden(0)
+        copy_hidden(0, 0)
+        copy_hidden(0, 1)
+        find_lacking(0)
         w3_codes = keep.tile([P, D], U32, align_bytes=64)
         w3_scales = keep.tile([P, D], U8, align_bytes=64)
-        w3_grouped = flip_rows(nc, nc.vector.tensor_copy, psum_flip, stage, ident_f32, w3_nat[:])
         quantise_rows(nc, w3_grouped, w3_codes[:], w3_scales[:])
-        scale_fields(0, 0)
-        flip_hidden(0)
-        scale_fields(0, 1)
+        for t in range(PACK):
+            scale_fields(0, t)
+        ow_banks = flip_weight(psum_second, "acc", ow_nat[:], alternate_words)
+        quantise_hidden(0)
+        ow_grouped = copy_weight(ow_banks)
+        sum_fields(1)
+        first_product(0)
+        first_product(1)
+        find_gains(1)
         ow_codes = keep.tile([P, D], U32, align_bytes=64)
         ow_scales = keep.tile([P, D], U8, align_bytes=64)
-        ow_grouped = flip_rows(nc, nc.vector.tensor_copy, psum_flip, stage, ident_f32, ow_nat[:])
-        quantise_hidden(0)
-        first_product(0)
         quantise_rows(nc, ow_grouped, ow_codes[:], ow_scales[:])
-        spread_out_b = psum_second.tile([P, D], F32, tag="bank")
+        flip_hidden(1)
+        spread_out_b = psum_second.tile([P, D], F32, tag="acc")
         nc.tensor.matmul(out=spread_out_b[:], lhsT=ones[:], rhs=out_b_row[:], start=True, stop=True)
         out_b_all = keep.tile([P, D], F32)
         nc.scalar.copy(out=out_b_all[:], in_=spread_out_b[:])
-        mend_last_tokens(0)
 
-        ALL = B * TILES
         for g in range(ALL + 2):
+            early = batch_due(g, 6)
+            if early is not None:
+                sum_fields(early)
+            if batch_due(g, 5) is not None:
+                flip_hidden(batch_due(g, 5))
+            if batch_due(g, 4) is not None:
+                flip_fields(batch_due(g, 4))
             if g < ALL:
                 fuse(g)
-            if g + 1 < ALL:
-                first_product(g + 1)
+                if g % TILES == 0:
+                    mend_last_tokens(g // TILES)
             if 0 <= g - 1 < ALL:
                 quantise_enhanced(g - 1)
                 second_product(g - 1)
+            if batch_due(g, 2) is not None:
+                quantise_hidden(batch_due(g, 2))
+            if g + 2 < ALL:
+                first_product(g + 2)
+            if batch_due(g, 4) is not None:
+                copy_hidden(batch_due(g, 4), 0)
+                copy_hidden(batch_due(g, 4), 1)
+            if batch_due(g, 3) is not None:
+                scale_fields(batch_due(g, 3), 0)
+                scale_fields(batch_due(g, 3), 1)
+            if batch_due(g, 2) is not None:
+                scale_fields(batch_due(g, 2), 2)
+            if batch_due(g, 1) is not None:
+                scale_fields(batch_due(g, 1), 3)
             if 0 <= g - 2 < ALL:
                 finish(g - 2)
-            if g == 0:
-                find_gains(1, B - 1)
-            if g // TILES + 1 < B:
-                prepare(g // TILES + 1, g % TILES)
+            if batch_due(g, 3) is not None:
+                find_lacking(batch_due(g, 3))
+            if early is not None:
+                find_gains(early)

@@ -16,7 +16,7 @@ P = 128
 PACK = 4
 TILES = 4
 ALL = B * TILES
-SCALAR_TILES = (0, 2)
+SCALAR_TILES = ()
 
 FLOPS = 2 * 2 * B * N * D * D
 

@@ -70,15 +70,19 @@ def tile_fieldinteractionoperators_pa_kernel(
         make_identity(nc, ident_f32[:])
         ones = keep.tile([P, P], BF16)
         nc.vector.memset(ones[:], 1.0)
-        ones_but_first = keep.tile([P, P], BF16)
-        nc.vector.memset(ones_but_first[:], 1.0)
-        nc.vector.memset(ones_but_first[0:1, :], 0.0)
         out_b_row = keep.tile([P, D], BF16)
         nc.vector.memset(out_b_row[:], 0.0)
         zero = keep.tile([P, 1], F32)
         nc.vector.memset(zero[:], 0.0)
+        token_weights = keep.tile([P, TILES, 2 * L], BF16)
+        nc.vector.memset(token_weights[:], 0.0)
+        nc.vector.memset(token_weights[:, :, 0:L], 1.0)
+        for s in range(L):
+            nc.vector.memset(token_weights[0:1, 0 : L - s, s : s + 1], 0.0)
+        for a in range(L):
+            nc.vector.tensor_copy(out=token_weights[:, a + 1, L + a : L + a + 1], in_=ident_f32[:, P - 1 : P])
 
-        kernels_all = keep.tile([P, H, L, L], BF16)
+        kernels_all = keep.tile([P, H, L * L], BF16)
         mix = keep.tile([P, 2], BF16)
         b3_pt = keep.tile([P, PACK], BF16)
         f_nat = keep.tile([P, B, TILES, D], BF16)
@@ -90,7 +94,7 @@ def tile_fieldinteractionoperators_pa_kernel(
             nc.sync.dma_start(out=tile[:, b], in_=tensor[b].rearrange("(q i) c -> q i c", i=TILES))
 
         nc.scalar.dma_start(
-            out=kernels_all[:].rearrange("p h l j -> p (h l j)"),
+            out=kernels_all[:].rearrange("p h x -> p (h x)"),
             in_=corr_kernels.rearrange("h l j -> (h l j)").partition_broadcast(P),
         )
         nc.scalar.dma_start(out=mix[:], in_=inter_w.partition_broadcast(P))
@@ -115,20 +119,24 @@ def tile_fieldinteractionoperators_pa_kernel(
         nc.scalar.activation(out=expd[:], in_=mix[:], func=ACT.Exp, bias=neg_top[:, 0:1], scale=1.0, accum_out=total[:])
 
         own_head = ident_f32[:].rearrange("p (h r) -> p h r", r=P // H)[:, :, 0]
-        pick = keep.tile([P, L, L + 1, L, H], F32)
-        nc.vector.memset(pick[:], 0.0)
+        by_head = keep.tile([P, L * L, H], F32)
+        nc.vector.tensor_tensor(
+            out=by_head[:],
+            in0=kernels_all[:].rearrange("p h x -> p x h"),
+            in1=own_head.unsqueeze(1).to_broadcast([P, L * L, H]),
+            op=ALU.mult,
+        )
+        kernels_own = keep.tile([P, L, L], F32)
+        nc.vector.tensor_reduce(out=kernels_own[:].rearrange("p l j -> p (l j)"), in_=by_head[:], axis=AXIS.X, op=ALU.add)
+        kappa = keep.tile([P, L, L + 1, L], F32)
+        nc.vector.memset(kappa[:], 0.0)
         for s in range(L):
             lag = L - s
-            nc.vector.scalar_tensor_tensor(
-                out=pick[:, :, L, s, :],
-                in0=kernels_all[:, :, lag - 1, :].rearrange("p h j -> p j h"),
-                scalar=1.0 / (L * (N - lag)),
-                in1=own_head.unsqueeze(1).to_broadcast([P, L, H]),
-                op0=ALU.mult,
-                op1=ALU.mult,
+            nc.vector.tensor_scalar_mul(
+                out=kappa[:, :, L, s], in0=kernels_own[:, lag - 1, :], scalar1=1.0 / (L * (N - lag))
             )
         for a in range(L):
-            nc.vector.tensor_copy(out=pick[:, :, a, 0 : a + 1, :], in_=pick[:, :, L, 0 : a + 1, :])
+            nc.vector.tensor_copy(out=kappa[:, :, a, 0 : a + 1], in_=kappa[:, :, L, 0 : a + 1])
         one_if_whole = keep.tile([P, L, L + 1], F32)
         nc.vector.memset(one_if_whole[:], 0.0)
         nc.vector.memset(one_if_whole[:, :, L : L + 1], 1.0)
@@ -141,38 +149,50 @@ def tile_fieldinteractionoperators_pa_kernel(
 
         gains = keep.tile([P, B, L, L + 1], F32)
         sums = {}
+        terms = {}
+        factors = {}
+        lacking = {}
 
         def sum_fields(b):
-            bank = psum_flip.tile([P, L * H, L], F32, tag="flipped")
-            for s in range(L):
-                lag = L - s
+            bank = psum_flip.tile([P, L, 2 * L], F32, tag="flipped")
+            for t in range(L):
                 for i in range(TILES):
                     nc.tensor.matmul(
-                        out=bank[:, s * H : (s + 1) * H, :],
-                        lhsT=ones[:] if i >= lag else ones_but_first[:],
-                        rhs=f_nat[:, b, i, :].rearrange("q (h j) -> q h j", j=HD)[:, :, 0:L],
+                        out=bank[:, t, :],
+                        lhsT=f_nat[:, b, i, :].rearrange("q (p t) -> q t p", t=PACK)[:, t, :],
+                        rhs=token_weights[:, i, :],
                         start=(i == 0),
                         stop=(i == TILES - 1),
                     )
             sums[b] = bank
 
-        def find_gains(b):
-            terms = stage.tile([P, L, L + 1, L * H], F32, tag="terms")
+        def weigh_sums(b):
+            weighed = stage.tile([P, L, L + 1, L], F32, tag="terms")
             nc.vector.tensor_tensor(
-                out=terms[:],
-                in0=sums[b][:].rearrange("p x j -> p j x").unsqueeze(2).to_broadcast([P, L, L + 1, L * H]),
-                in1=pick[:].rearrange("p j a s h -> p j a (s h)"),
+                out=weighed[:],
+                in0=sums[b][:, :, 0:L].unsqueeze(2).to_broadcast([P, L, L + 1, L]),
+                in1=kappa[:],
                 op=ALU.mult,
             )
-            factors = stage.tile([P, L, L + 1], F32, tag="factors")
-            nc.vector.tensor_reduce(out=factors[:], in_=terms[:], axis=AXIS.X, op=ALU.add)
+            terms[b] = weighed
+
+        def add_terms(b):
+            added = stage.tile([P, L, L + 1], F32, tag="factors")
+            nc.vector.tensor_reduce(out=added[:], in_=terms[b][:], axis=AXIS.X, op=ALU.add)
+            factors[b] = added
+
+        def make_gains(b):
             nc.vector.scalar_tensor_tensor(
-                out=gains[:, b], in0=factors[:], scalar=iw[:, 0:1], in1=one_if_whole[:], op0=ALU.mult, op1=ALU.add
+                out=gains[:, b], in0=factors[b][:], scalar=iw[:, 0:1], in1=one_if_whole[:], op0=ALU.mult, op1=ALU.add
             )
+
+        def find_lacking(b):
+            lack = stage.tile([P, L, L], F32, tag="lacking")
+            nc.vector.tensor_tensor(out=lack[:], in0=sums[b][:, :, L : 2 * L], in1=gains[:, b, :, 0:L], op=ALU.mult)
+            lacking[b] = lack
 
         field_banks = {}
         scaled = {}
-        lacking = {}
         hidden_banks = {}
         h_grouped = {}
         h_codes = {}
@@ -198,19 +218,6 @@ def tile_fieldinteractionoperators_pa_kernel(
                 bias=bias_pt[:, t : t + 1],
             )
 
-        def find_lacking(b):
-            lack = stage.tile([P, L, L], F32, tag="lacking")
-            for u in range(2):
-                count = min(2, L - 2 * u)
-                halves = field_banks[(b, u)][:].bitcast(BF16).rearrange("p i (q e) -> p e i q", e=2)
-                nc.vector.tensor_tensor(
-                    out=lack[:, 2 * u : 2 * u + count, :],
-                    in0=halves[:, 0:count, 1:TILES, P - 1],
-                    in1=gains[:, b, 2 * u : 2 * u + count, 0:L],
-                    op=ALU.mult,
-                )
-            lacking[b] = lack
-
         def mend_last_tokens(b):
             last_columns = scaled[b][:, 0:L, :].rearrange("p t (i q) -> p t i q", q=P)[:, :, 1:TILES, P - 1]
             nc.vector.tensor_tensor(out=last_columns, in0=last_columns, in1=lacking[b][:], op=ALU.subtract)
@@ -223,8 +230,8 @@ def tile_fieldinteractionoperators_pa_kernel(
             grouped = stage.tile([P, TILES, P, PACK], BF16, align_bytes=64, tag="grouped")
             h_grouped[b] = grouped
 
-        def copy_hidden(b, pair):
-            copy_two_row_tiles(nc.scalar.copy, h_grouped[b], pair, hidden_banks[(b, pair)])
+        def copy_hidden(copy_out, b, pair):
+            copy_two_row_tiles(copy_out, h_grouped[b], pair, hidden_banks[(b, pair)])
 
         def quantise_hidden(b):
             codes = stage.tile([P, N], U32, align_bytes=64, tag="h_codes")
@@ -243,7 +250,7 @@ def tile_fieldinteractionoperators_pa_kernel(
         def copy_weight(banks):
             grouped = stage.tile([P, TILES, P, PACK], BF16, align_bytes=64, tag="grouped")
             for pair in range(2):
-                copy_two_row_tiles(nc.vector.tensor_copy, grouped, pair, banks[pair])
+                copy_two_row_tiles(nc.scalar.copy, grouped, pair, banks[pair])
             return grouped
 
         nl = {}
@@ -251,7 +258,6 @@ def tile_fieldinteractionoperators_pa_kernel(
         e_codes = {}
         e_scales = {}
         acc = {}
-        result = {}
 
         def first_product(g):
             b, i = divmod(g, TILES)
@@ -306,72 +312,83 @@ def tile_fieldinteractionoperators_pa_kernel(
 
         def finish(g):
             b, i = divmod(g, TILES)
-            if i % 2 == 0:
-                both = results.tile([P, 2, D], F32, tag="both")
-                result[g] = result[g + 1] = both
-            mine = result[g][:, i % 2, :]
+            result = results.tile([P, D], F32, tag="result")
             if i in SCALAR_TILES:
-                nc.scalar.copy(out=mine, in_=acc[g][:])
-                nc.gpsimd.tensor_tensor(out=mine, in0=mine, in1=out_b_all[:], op=ALU.add)
+                nc.scalar.copy(out=result[:], in_=acc[g][:])
+                nc.gpsimd.tensor_tensor(out=result[:], in0=result[:], in1=out_b_all[:], op=ALU.add)
             else:
-                nc.vector.tensor_tensor(out=mine, in0=acc[g][:], in1=out_b_all[:], op=ALU.add)
-            if i % 2 == 1:
-                nc.sync.dma_start(
-                    out=out[b].rearrange("(q i) o -> q i o", i=TILES)[:, i - 1 : i + 1, :], in_=result[g][:]
-                )
+                nc.vector.tensor_tensor(out=result[:], in0=acc[g][:], in1=out_b_all[:], op=ALU.add)
+            nc.sync.dma_start(out=out[b].rearrange("(q i) o -> q i o", i=TILES)[:, i, :], in_=result[:])
 
         sum_fields(0)
-        find_gains(0)
-        flip_fields(0)
+        weigh_sums(0)
+        add_terms(0)
+        make_gains(0)
+        find_lacking(0)
         w3_banks = flip_weight(psum_first, "nl", w3_nat[:], near_words)
         w3_grouped = copy_weight(w3_banks)
+        flip_fields(0)
+        for t in range(PACK):
+            scale_fields(0, t)
         flip_hidden(0)
-        copy_hidden(0, 0)
-        copy_hidden(0, 1)
-        find_lacking(0)
         w3_codes = keep.tile([P, D], U32, align_bytes=64)
         w3_scales = keep.tile([P, D], U8, align_bytes=64)
         quantise_rows(nc, w3_grouped, w3_codes[:], w3_scales[:])
-        for t in range(PACK):
-            scale_fields(0, t)
-        ow_banks = flip_weight(psum_second, "acc", ow_nat[:], alternate_words)
-        quantise_hidden(0)
-        ow_grouped = copy_weight(ow_banks)
+        copy_hidden(nc.vector.tensor_copy, 0, 0)
+        copy_hidden(nc.vector.tensor_copy, 0, 1)
         sum_fields(1)
+        quantise_hidden(0)
+        weigh_sums(1)
+        ow_banks = flip_weight(psum_second, "acc", ow_nat[:], alternate_words)
+        ow_grouped = copy_weight(ow_banks)
         first_product(0)
         first_product(1)
-        find_gains(1)
-        ow_codes = keep.tile([P, D], U32, align_bytes=64)
-        ow_scales = keep.tile([P, D], U8, align_bytes=64)
-        quantise_rows(nc, ow_grouped, ow_codes[:], ow_scales[:])
-        flip_hidden(1)
+        add_terms(1)
+        make_gains(1)
         spread_out_b = psum_second.tile([P, D], F32, tag="acc")
         nc.tensor.matmul(out=spread_out_b[:], lhsT=ones[:], rhs=out_b_row[:], start=True, stop=True)
         out_b_all = keep.tile([P, D], F32)
         nc.scalar.copy(out=out_b_all[:], in_=spread_out_b[:])
+        fuse(0)
+        find_lacking(1)
+        flip_hidden(1)
+        flip_fields(1)
+        ow_codes = keep.tile([P, D], U32, align_bytes=64)
+        ow_scales = keep.tile([P, D], U8, align_bytes=64)
+        quantise_rows(nc, ow_grouped, ow_codes[:], ow_scales[:])
+        mend_last_tokens(0)
+        first_product(2)
+        copy_hidden(nc.scalar.copy, 1, 0)
+        copy_hidden(nc.scalar.copy, 1, 1)
 
-        for g in range(ALL + 2):
-            early = batch_due(g, 6)
-            if early is not None:
-                sum_fields(early)
+        for g in range(1, ALL + 2):
+            if g < ALL:
+                fuse(g)
+            if g < ALL and g % TILES == 0:
+                mend_last_tokens(g // TILES)
+            if batch_due(g, 6) is not None:
+                weigh_sums(batch_due(g, 6))
             if batch_due(g, 5) is not None:
+                find_lacking(batch_due(g, 5))
                 flip_hidden(batch_due(g, 5))
             if batch_due(g, 4) is not None:
                 flip_fields(batch_due(g, 4))
-            if g < ALL:
-                fuse(g)
-                if g % TILES == 0:
-                    mend_last_tokens(g // TILES)
-            if 0 <= g - 1 < ALL:
+            if g - 1 < ALL:
                 quantise_enhanced(g - 1)
                 second_product(g - 1)
+            if batch_due(g, 6) is not None:
+                add_terms(batch_due(g, 6))
             if batch_due(g, 2) is not None:
                 quantise_hidden(batch_due(g, 2))
             if g + 2 < ALL:
                 first_product(g + 2)
+            if batch_due(g, 7) is not None:
+                sum_fields(batch_due(g, 7))
+            if g - 2 >= 0:
+                finish(g - 2)
             if batch_due(g, 4) is not None:
-                copy_hidden(batch_due(g, 4), 0)
-                copy_hidden(batch_due(g, 4), 1)
+                copy_hidden(nc.scalar.copy, batch_due(g, 4), 0)
+                copy_hidden(nc.scalar.copy, batch_due(g, 4), 1)
             if batch_due(g, 3) is not None:
                 scale_fields(batch_due(g, 3), 0)
                 scale_fields(batch_due(g, 3), 1)
@@ -379,9 +396,5 @@ def tile_fieldinteractionoperators_pa_kernel(
                 scale_fields(batch_due(g, 2), 2)
             if batch_due(g, 1) is not None:
                 scale_fields(batch_due(g, 1), 3)
-            if 0 <= g - 2 < ALL:
-                finish(g - 2)
-            if batch_due(g, 3) is not None:
-                find_lacking(batch_due(g, 3))
-            if early is not None:
-                find_gains(early)
+            if batch_due(g, 6) is not None:
+                make_gains(batch_due(g, 6))

@@ -349,19 +349,21 @@ def tile_fieldinteractionoperators_pa_kernel(
         nc.tensor.matmul(out=spread_out_b[:], lhsT=ones[:], rhs=out_b_row[:], start=True, stop=True)
         out_b_all = keep.tile([P, D], F32)
         nc.scalar.copy(out=out_b_all[:], in_=spread_out_b[:])
-        fuse(0)
         find_lacking(1)
         flip_hidden(1)
+        fuse(0)
+        first_product(2)
         flip_fields(1)
         ow_codes = keep.tile([P, D], U32, align_bytes=64)
         ow_scales = keep.tile([P, D], U8, align_bytes=64)
         quantise_rows(nc, ow_grouped, ow_codes[:], ow_scales[:])
         mend_last_tokens(0)
-        first_product(2)
         copy_hidden(nc.scalar.copy, 1, 0)
         copy_hidden(nc.scalar.copy, 1, 1)
 
         for g in range(1, ALL + 2):
+            if batch_due(g, 7) is not None:
+                sum_fields(batch_due(g, 7))
             if g < ALL:
                 fuse(g)
             if g < ALL and g % TILES == 0:
@@ -378,12 +380,10 @@ def tile_fieldinteractionoperators_pa_kernel(
                 second_product(g - 1)
             if batch_due(g, 6) is not None:
                 add_terms(batch_due(g, 6))
-            if batch_due(g, 2) is not None:
-                quantise_hidden(batch_due(g, 2))
+            if batch_due(g, 3) is not None:
+                quantise_hidden(batch_due(g, 3))
             if g + 2 < ALL:
                 first_product(g + 2)
-            if batch_due(g, 7) is not None:
-                sum_fields(batch_due(g, 7))
             if g - 2 >= 0:
                 finish(g - 2)
             if batch_due(g, 4) is not None:

@@ -137,20 +137,19 @@ def tile_fieldinteractionoperators_pa_kernel(
             )
         for a in range(L):
             nc.vector.tensor_copy(out=kappa[:, :, a, 0 : a + 1], in_=kappa[:, :, L, 0 : a + 1])
-        one_if_whole = keep.tile([P, L, L + 1], F32)
-        nc.vector.memset(one_if_whole[:], 0.0)
-        nc.vector.memset(one_if_whole[:, :, L : L + 1], 1.0)
+        terms = keep.tile([P, L, L + 1, L + 1], F32)
+        nc.vector.memset(terms[:], 0.0)
+        nc.vector.memset(terms[:, :, L, L : L + 1], 1.0)
 
         nc.vector.reciprocal(out=total[:], in_=total[:])
         iw = keep.tile([P, 2], F32)
         nc.vector.tensor_scalar_mul(out=iw[:], in0=expd[:], scalar1=total[:, 0:1])
         bias_pt = keep.tile([P, PACK], F32)
         nc.vector.tensor_scalar_mul(out=bias_pt[:], in0=b3_pt[:], scalar1=iw[:, 1:2])
+        nc.vector.tensor_scalar_mul(out=kappa[:], in0=kappa[:], scalar1=iw[:, 0:1])
 
         gains = keep.tile([P, B, L, L + 1], F32)
         sums = {}
-        terms = {}
-        factors = {}
         lacking = {}
 
         def sum_fields(b):
@@ -167,24 +166,15 @@ def tile_fieldinteractionoperators_pa_kernel(
             sums[b] = bank
 
         def weigh_sums(b):
-            weighed = stage.tile([P, L, L + 1, L], F32, tag="terms")
             nc.vector.tensor_tensor(
-                out=weighed[:],
+                out=terms[:, :, :, 0:L],
                 in0=sums[b][:, :, 0:L].unsqueeze(2).to_broadcast([P, L, L + 1, L]),
                 in1=kappa[:],
                 op=ALU.mult,
             )
-            terms[b] = weighed
 
         def add_terms(b):
-            added = stage.tile([P, L, L + 1], F32, tag="factors")
-            nc.vector.tensor_reduce(out=added[:], in_=terms[b][:], axis=AXIS.X, op=ALU.add)
-            factors[b] = added
-
-        def make_gains(b):
-            nc.vector.scalar_tensor_tensor(
-                out=gains[:, b], in0=factors[b][:], scalar=iw[:, 0:1], in1=one_if_whole[:], op0=ALU.mult, op1=ALU.add
-            )
+            nc.vector.tensor_reduce(out=gains[:, b], in_=terms[:], axis=AXIS.X, op=ALU.add)
 
         def find_lacking(b):
             lack = stage.tile([P, L, L], F32, tag="lacking")
@@ -323,7 +313,6 @@ def tile_fieldinteractionoperators_pa_kernel(
         sum_fields(0)
         weigh_sums(0)
         add_terms(0)
-        make_gains(0)
         find_lacking(0)
         w3_banks = flip_weight(psum_first, "nl", w3_nat[:], near_words)
         w3_grouped = copy_weight(w3_banks)
@@ -336,15 +325,14 @@ def tile_fieldinteractionoperators_pa_kernel(
         quantise_rows(nc, w3_grouped, w3_codes[:], w3_scales[:])
         copy_hidden(nc.vector.tensor_copy, 0, 0)
         copy_hidden(nc.vector.tensor_copy, 0, 1)
+        ow_banks = flip_weight(psum_second, "acc", ow_nat[:], alternate_words)
+        ow_grouped = copy_weight(ow_banks)
         sum_fields(1)
         quantise_hidden(0)
         weigh_sums(1)
-        ow_banks = flip_weight(psum_second, "acc", ow_nat[:], alternate_words)
-        ow_grouped = copy_weight(ow_banks)
         first_product(0)
         first_product(1)
         add_terms(1)
-        make_gains(1)
         spread_out_b = psum_second.tile([P, D], F32, tag="acc")
         nc.tensor.matmul(out=spread_out_b[:], lhsT=ones[:], rhs=out_b_row[:], start=True, stop=True)
         out_b_all = keep.tile([P, D], F32)
@@ -396,5 +384,3 @@ def tile_fieldinteractionoperators_pa_kernel(
                 scale_fields(batch_due(g, 2), 2)
             if batch_due(g, 1) is not None:
                 scale_fields(batch_due(g, 1), 3)
-            if batch_due(g, 6) is not None:
-                make_gains(batch_due(g, 6))

@@ -64,7 +64,6 @@ def tile_fieldinteractionoperators_pa_kernel(
         tc.psum_pool(name="psum_field", bufs=2) as psum_field,
         tc.psum_pool(name="psum_first", bufs=2) as psum_first,
         tc.psum_pool(name="psum_second", bufs=2) as psum_second,
-        tc.manual_schedule(),
     ):
         ident_f32 = keep.tile([P, P], F32)
         make_identity(nc, ident_f32[:])

import concourse.mybir as mybir
from concourse.masks import make_identity

F32 = mybir.dt.float32
BF16 = mybir.dt.bfloat16
U32 = mybir.dt.uint32
U8 = mybir.dt.uint8
FP8X4 = mybir.dt.float8_e4m3fn_x4
ALU = mybir.AluOpType
ACT = mybir.ActivationFunctionType
AXIS = mybir.AxisListType

B, N, D, H, L = 4, 512, 512, 8, 3
HD = D // H
P = 128
PACK = 4
TILES = 4
ALL = B * TILES
SCALAR_TILES = ()

FLOPS = 2 * 2 * B * N * D * D


def near_words(rows, u):
    return rows.bitcast(F32)[:, u * P : (u + 1) * P]


def alternate_words(rows, u):
    return rows.bitcast(F32).rearrange("r (p u) -> r u p", u=2)[:, u, :]


def flip_two_row_tiles(nc, bank, rows2, words, ident_f32):
    for g in range(2):
        for u in range(2):
            nc.tensor.transpose(bank[:, g, u, :], words(rows2[:, g, :], u), ident_f32[:])


def copy_two_row_tiles(copy_out, grouped, pair, bank):
    copy_out(
        out=grouped[:].bitcast(F32)[:, 2 * pair : 2 * pair + 2, :, :], in_=bank[:].rearrange("p g u r -> p g r u")
    )


def quantise_rows(nc, grouped, codes, scales):
    nc.vector.quantize_mx(
        out=codes.bitcast(FP8X4), scales=scales, in_=grouped[:].rearrange("p g r t -> p (g r t)")
    )


def batch_due(g, lead):
    b, rest = divmod(g + lead, TILES)
    return b if rest == 0 and b < B else None


def tile_fieldinteractionoperators_pa_kernel(
    tc, fields, h2, corr_kernels, w3, b3, out_w, out_b, inter_w, out
):
    nc = tc.nc
    with (
        tc.tile_pool(name="keep", bufs=1) as keep,
        tc.tile_pool(name="stage", bufs=2) as stage,
        tc.tile_pool(name="results", bufs=4) as results,
        tc.psum_pool(name="psum_flip", bufs=2) as psum_flip,
        tc.psum_pool(name="psum_field", bufs=2) as psum_field,
        tc.psum_pool(name="psum_first", bufs=2) as psum_first,
        tc.psum_pool(name="psum_second", bufs=2) as psum_second,
    ):
        ident_f32 = keep.tile([P, P], F32)
        make_identity(nc, ident_f32[:])
        ones = keep.tile([P, P], BF16)
        nc.vector.memset(ones[:], 1.0)
        out_b_row = keep.tile([P, D], BF16)
        nc.vector.memset(out_b_row[:], 0.0)
        zero = keep.tile([P, 1], F32)
        nc.vector.memset(zero[:], 0.0)
        token_weights = keep.tile([P, TILES, 2 * L], BF16)
        nc.vector.memset(token_weights[:], 0.0)
        nc.vector.memset(token_weights[:, :, 0:L], 1.0)
        for s in range(L):
            nc.vector.memset(token_weights[0:1, 0 : L - s, s : s + 1], 0.0)
        for a in range(L):
            nc.vector.tensor_copy(out=token_weights[:, a + 1, L + a : L + a + 1], in_=ident_f32[:, P - 1 : P])

        kernels_all = keep.tile([P, H, L * L], BF16)
        mix = keep.tile([P, 2], BF16)
        b3_pt = keep.tile([P, PACK], BF16)
        f_nat = keep.tile([P, B, TILES, D], BF16)
        h_nat = keep.tile([P, B, TILES, D], BF16)
        w3_nat = keep.tile([P, TILES, D], BF16)
        ow_nat = keep.tile([P, TILES, D], BF16)

        def load_tokens(tile, tensor, b):
            nc.sync.dma_start(out=tile[:, b], in_=tensor[b].rearrange("(q i) c -> q i c", i=TILES))

        nc.scalar.dma_start(
            out=kernels_all[:].rearrange("p h x -> p (h x)"),
            in_=corr_kernels.rearrange("h l j -> (h l j)").partition_broadcast(P),
        )
        nc.scalar.dma_start(out=mix[:], in_=inter_w.partition_broadcast(P))
        nc.scalar.dma_start(out=b3_pt[:], in_=b3.rearrange("(p t) -> p t", t=PACK))
        nc.scalar.dma_start(out=out_b_row[0:1, :], in_=out_b.unsqueeze(0))
        load_tokens(f_nat, fields, 0)
        nc.sync.dma_start(out=w3_nat[:], in_=w3.rearrange("(p t) k -> p t k", t=TILES))
        load_tokens(h_nat, h2, 0)
        nc.sync.dma_start(out=ow_nat[:], in_=out_w.rearrange("(g r) c -> r g c", r=P))
        for b in range(1, B):
            load_tokens(f_nat, fields, b)
            load_tokens(h_nat, h2, b)

        warm = keep.tile([P, 1], F32)
        nc.scalar.activation(out=warm[:], in_=zero[:], func=ACT.Exp)

        neg_top = keep.tile([P, 1], F32)
        nc.vector.tensor_max(out=neg_top[:], in0=mix[:, 0:1], in1=mix[:, 1:2])
        nc.vector.tensor_scalar_mul(out=neg_top[:], in0=neg_top[:], scalar1=-1.0)
        expd = keep.tile([P, 2], F32)
        total = keep.tile([P, 1], F32)
        nc.scalar.activation(out=expd[:], in_=mix[:], func=ACT.Exp, bias=neg_top[:, 0:1], scale=1.0, accum_out=total[:])

        own_head = ident_f32[:].rearrange("p (h r) -> p h r", r=P // H)[:, :, 0]
        by_head = keep.tile([P, L * L, H], F32)
        nc.vector.tensor_tensor(
            out=by_head[:],
            in0=kernels_all[:].rearrange("p h x -> p x h"),
            in1=own_head.unsqueeze(1).to_broadcast([P, L * L, H]),
            op=ALU.mult,
        )
        kernels_own = keep.tile([P, L, L], F32)
        nc.vector.tensor_reduce(out=kernels_own[:].rearrange("p l j -> p (l j)"), in_=by_head[:], axis=AXIS.X, op=ALU.add)
        kappa = keep.tile([P, L, L + 1, L], F32)
        nc.vector.memset(kappa[:], 0.0)
        for s in range(L):
            lag = L - s
            nc.vector.tensor_scalar_mul(
                out=kappa[:, :, L, s], in0=kernels_own[:, lag - 1, :], scalar1=1.0 / (L * (N - lag))
            )
        for a in range(L):
            nc.vector.tensor_copy(out=kappa[:, :, a, 0 : a + 1], in_=kappa[:, :, L, 0 : a + 1])
        terms = keep.tile([P, L, L + 1, L + 1], F32)
        nc.vector.memset(terms[:], 0.0)
        nc.vector.memset(terms[:, :, L, L : L + 1], 1.0)

        nc.vector.reciprocal(out=total[:], in_=total[:])
        iw = keep.tile([P, 2], F32)
        nc.vector.tensor_scalar_mul(out=iw[:], in0=expd[:], scalar1=total[:, 0:1])
        bias_pt = keep.tile([P, PACK], F32)
        nc.vector.tensor_scalar_mul(out=bias_pt[:], in0=b3_pt[:], scalar1=iw[:, 1:2])
        nc.vector.tensor_scalar_mul(out=kappa[:], in0=kappa[:], scalar1=iw[:, 0:1])

        gains = keep.tile([P, B, L, L + 1], F32)
        sums = {}
        lacking = {}

        def sum_fields(b):
            bank = psum_flip.tile([P, L, 2 * L], F32, tag="flipped")
            for t in range(L):
                for i in range(TILES):
                    nc.tensor.matmul(
                        out=bank[:, t, :],
                        lhsT=f_nat[:, b, i, :].rearrange("q (p t) -> q t p", t=PACK)[:, t, :],
                        rhs=token_weights[:, i, :],
                        start=(i == 0),
                        stop=(i == TILES - 1),
                    )
            sums[b] = bank

        def weigh_sums(b):
            nc.vector.tensor_tensor(
                out=terms[:, :, :, 0:L],
                in0=sums[b][:, :, 0:L].unsqueeze(2).to_broadcast([P, L, L + 1, L]),
                in1=kappa[:],
                op=ALU.mult,
            )

        def add_terms(b):
            nc.vector.tensor_reduce(out=gains[:, b], in_=terms[:], axis=AXIS.X, op=ALU.add)

        def find_lacking(b):
            lack = stage.tile([P, L, L], F32, tag="lacking")
            nc.vector.tensor_tensor(out=lack[:], in0=sums[b][:, :, L : 2 * L], in1=gains[:, b, :, 0:L], op=ALU.mult)
            lacking[b] = lack

        field_banks = {}
        scaled = {}
        hidden_banks = {}
        h_grouped = {}
        h_codes = {}
        h_scales = {}

        def flip_fields(b):
            for u in range(2):
                flipped_f = psum_field.tile([P, TILES, P], F32, tag="fields")
                for i in range(TILES):
                    nc.tensor.transpose(flipped_f[:, i, :], alternate_words(f_nat[:, b, i, :], u), ident_f32[:])
                field_banks[(b, u)] = flipped_f
            scaled_b = stage.tile([P, PACK, N], F32, tag="scaled")
            scaled[b] = scaled_b

        def scale_fields(b, t):
            u, e = divmod(t, 2)
            halves = field_banks[(b, u)][:].bitcast(BF16).rearrange("p i (q e) -> p (i q) e", e=2)
            nc.scalar.activation(
                out=scaled[b][:, t, :],
                in_=halves[:, :, e],
                func=ACT.Identity,
                scale=gains[:, b, t, L : L + 1] if t < L else 1.0,
                bias=bias_pt[:, t : t + 1],
            )

        def mend_last_tokens(b):
            last_columns = scaled[b][:, 0:L, :].rearrange("p t (i q) -> p t i q", q=P)[:, :, 1:TILES, P - 1]
            nc.vector.tensor_tensor(out=last_columns, in0=last_columns, in1=lacking[b][:], op=ALU.subtract)

        def flip_hidden(b):
            for pair in range(2):
                bank = psum_flip.tile([P, 2, 2, P], F32, tag="flipped")
                flip_two_row_tiles(nc, bank, h_nat[:, b, 2 * pair : 2 * pair + 2, :], near_words, ident_f32)
                hidden_banks[(b, pair)] = bank
            grouped = stage.tile([P, TILES, P, PACK], BF16, align_bytes=64, tag="grouped")
            h_grouped[b] = grouped

        def copy_hidden(copy_out, b, pair):
            copy_two_row_tiles(copy_out, h_grouped[b], pair, hidden_banks[(b, pair)])

        def quantise_hidden(b):
            codes = stage.tile([P, N], U32, align_bytes=64, tag="h_codes")
            planes = stage.tile([P, N], U8, align_bytes=64, tag="h_scales")
            quantise_rows(nc, h_grouped[b], codes[:], planes[:])
            h_codes[b], h_scales[b] = codes, planes

        def flip_weight(pool, tag, rows4, words):
            banks = []
            for pair in range(2):
                bank = pool.tile([P, 2, 2, P], F32, tag=tag, name="weight_bank")
                flip_two_row_tiles(nc, bank, rows4[:, 2 * pair : 2 * pair + 2, :], words, ident_f32)
                banks.append(bank)
            return banks

        def copy_weight(banks):
            grouped = stage.tile([P, TILES, P, PACK], BF16, align_bytes=64, tag="grouped")
            for pair in range(2):
                copy_two_row_tiles(nc.scalar.copy, grouped, pair, banks[pair])
            return grouped

        nl = {}
        enhanced = {}
        e_codes = {}
        e_scales = {}
        acc = {}

        def first_product(g):
            b, i = divmod(g, TILES)
            tokens = slice(i * P, (i + 1) * P)
            bank = psum_first.tile([P, PACK, P], F32, tag="nl")
            for t in range(PACK):
                channels = slice(t * P, (t + 1) * P)
                nc.tensor.matmul_mx(
                    out=bank[:, t, :],
                    lhsT=w3_codes[:, channels].bitcast(FP8X4),
                    lhsT_scale=w3_scales[:, channels],
                    rhs=h_codes[b][:, tokens].bitcast(FP8X4),
                    rhs_scale=h_scales[b][:, tokens],
                    start=True,
                    stop=True,
                )
            nl[g] = bank

        def fuse(g):
            b, i = divmod(g, TILES)
            fused = results.tile([P, P, PACK], BF16, align_bytes=64, tag="fused")
            nc.vector.scalar_tensor_tensor(
                out=fused[:],
                in0=nl[g][:].rearrange("p t q -> p q t"),
                scalar=iw[:, 1:2],
                in1=scaled[b][:, :, i * P : (i + 1) * P].rearrange("p t q -> p q t"),
                op0=ALU.mult,
                op1=ALU.add,
            )
            enhanced[g] = fused

        def quantise_enhanced(g):
            codes = results.tile([P, P], U32, align_bytes=64, tag="e_codes")
            planes = results.tile([P, P], U8, align_bytes=64, tag="e_scales")
            nc.vector.quantize_mx(
                out=codes[:].bitcast(FP8X4), scales=planes[:], in_=enhanced[g][:].rearrange("p q t -> p (q t)")
            )
            e_codes[g], e_scales[g] = codes, planes

        def second_product(g):
            bank = psum_second.tile([P, D], F32, tag="acc")
            nc.tensor.matmul_mx(
                out=bank[:],
                lhsT=e_codes[g][:].bitcast(FP8X4),
                lhsT_scale=e_scales[g][:],
                rhs=ow_codes[:].bitcast(FP8X4),
                rhs_scale=ow_scales[:],
                start=True,
                stop=True,
            )
            acc[g] = bank

        def finish(g):
            b, i = divmod(g, TILES)
            result = results.tile([P, D], F32, tag="result")
            if i in SCALAR_TILES:
                nc.scalar.copy(out=result[:], in_=acc[g][:])
                nc.gpsimd.tensor_tensor(out=result[:], in0=result[:], in1=out_b_all[:], op=ALU.add)
            else:
                nc.vector.tensor_tensor(out=result[:], in0=acc[g][:], in1=out_b_all[:], op=ALU.add)
            nc.sync.dma_start(out=out[b].rearrange("(q i) o -> q i o", i=TILES)[:, i, :], in_=result[:])

        sum_fields(0)
        weigh_sums(0)
        add_terms(0)
        find_lacking(0)
        w3_banks = flip_weight(psum_first, "nl", w3_nat[:], near_words)
        w3_grouped = copy_weight(w3_banks)
        flip_fields(0)
        for t in range(PACK):
            scale_fields(0, t)
        flip_hidden(0)
        w3_codes = keep.tile([P, D], U32, align_bytes=64)
        w3_scales = keep.tile([P, D], U8, align_bytes=64)
        quantise_rows(nc, w3_grouped, w3_codes[:], w3_scales[:])
        copy_hidden(nc.vector.tensor_copy, 0, 0)
        copy_hidden(nc.vector.tensor_copy, 0, 1)
        ow_banks = flip_weight(psum_second, "acc", ow_nat[:], alternate_words)
        ow_grouped = copy_weight(ow_banks)
        sum_fields(1)
        quantise_hidden(0)
        weigh_sums(1)
        first_product(0)
        first_product(1)
        add_terms(1)
        spread_out_b = psum_second.tile([P, D], F32, tag="acc")
        nc.tensor.matmul(out=spread_out_b[:], lhsT=ones[:], rhs=out_b_row[:], start=True, stop=True)
        out_b_all = keep.tile([P, D], F32)
        nc.scalar.copy(out=out_b_all[:], in_=spread_out_b[:])
        find_lacking(1)
        flip_hidden(1)
        fuse(0)
        first_product(2)
        flip_fields(1)
        ow_codes = keep.tile([P, D], U32, align_bytes=64)
        ow_scales = keep.tile([P, D], U8, align_bytes=64)
        quantise_rows(nc, ow_grouped, ow_codes[:], ow_scales[:])
        mend_last_tokens(0)
        copy_hidden(nc.scalar.copy, 1, 0)
        copy_hidden(nc.scalar.copy, 1, 1)

        for g in range(1, ALL + 2):
            if batch_due(g, 7) is not None:
                sum_fields(batch_due(g, 7))
            if g < ALL:
                fuse(g)
            if g < ALL and g % TILES == 0:
                mend_last_tokens(g // TILES)
            if batch_due(g, 6) is not None:
                weigh_sums(batch_due(g, 6))
            if batch_due(g, 5) is not None:
                find_lacking(batch_due(g, 5))
                flip_hidden(batch_due(g, 5))
            if batch_due(g, 4) is not None:
                flip_fields(batch_due(g, 4))
            if g - 1 < ALL:
                quantise_enhanced(g - 1)
                second_product(g - 1)
            if batch_due(g, 6) is not None:
                add_terms(batch_due(g, 6))
            if batch_due(g, 3) is not None:
                quantise_hidden(batch_due(g, 3))
            if g + 2 < ALL:
                first_product(g + 2)
            if g - 2 >= 0:
                finish(g - 2)
            if batch_due(g, 4) is not None:
                copy_hidden(nc.scalar.copy, batch_due(g, 4), 0)
                copy_hidden(nc.scalar.copy, batch_due(g, 4), 1)
            if batch_due(g, 3) is not None:
                scale_fields(batch_due(g, 3), 0)
                scale_fields(batch_due(g, 3), 1)
            if batch_due(g, 2) is not None:
                scale_fields(batch_due(g, 2), 2)
            if batch_due(g, 1) is not None:
                scale_fields(batch_due(g, 1), 3)
